import numpy as np
import ml_dtypes


def mxq(x, axis, fmt="e4m3"):
    dtype, down = {"e4m3": (ml_dtypes.float8_e4m3fn, 7), "e5m2": (ml_dtypes.float8_e5m2, 14)}[fmt]
    v = np.moveaxis(np.asarray(x, np.float32).astype(ml_dtypes.bfloat16).astype(np.float64), axis, -1)
    blocks = v.reshape(v.shape[:-1] + (-1, 32))
    amax = np.abs(blocks).max(-1, keepdims=True)
    byte = np.maximum(np.where(amax > 0, np.frexp(amax)[1] - 1 + 127, 0) - down, 1)
    scale = np.exp2(byte - 127.0)
    codes = (blocks / scale).astype(np.float32).astype(dtype).astype(np.float64)
    return np.moveaxis((codes * scale).reshape(v.shape), -1, axis)


WIDE = False


def mx_kscale(k):
    if not WIDE:
        return np.ones(k)
    levels = np.array([20, -20, 10, -10, 0])
    a = np.random.permutation(np.resize(levels, k // 512 * 4)).reshape(k // 512, 4)
    idx = np.arange(k)
    return np.exp2(a[idx // 512, idx % 128 // 32])


BF16 = ml_dtypes.bfloat16


def bf(x):
    return np.asarray(x, np.float32).astype(BF16)


def f64(x):
    return np.asarray(x).astype(np.float64)


B, S, HID, NH, NOPE, ROPE, VD, KV_RANK, SW, QB = 1, 2048, 1024, 8, 64, 128, 128, 512, 384, 128
QK = NOPE + ROPE


def rotate_half(x):
    h = x.shape[-1] // 2
    return np.concatenate([-x[..., h:], x[..., :h]], axis=-1)


def rotate_half_t(x):
    h = x.shape[-1] // 2
    return np.concatenate([x[..., h:], -x[..., :h]], axis=-1)


def rope_tables():
    pos = np.arange(S, dtype=np.float64)
    inv = 1.0 / (10000.0 ** (np.arange(0, ROPE, 2, dtype=np.float64) / ROPE))
    ang = pos[:, None] * inv[None, :]
    ang = np.concatenate([ang, ang], axis=-1)
    return bf(np.broadcast_to(np.cos(ang)[None], (B, S, ROPE))), bf(np.broadcast_to(np.sin(ang)[None], (B, S, ROPE)))


def setup_inputs():
    s = mx_kscale(S)
    cos, sin = rope_tables()
    hs = np.random.standard_normal((B, S, HID)) * s[None, :, None]
    wq = np.random.standard_normal((HID, NH * QK)) * 2.0 / np.sqrt(HID)
    bq = np.random.standard_normal(NH * QK) * 0.2
    g = np.random.standard_normal((B, NH, S, QK)) * np.exp2(np.random.randint(-12, 1, (B, 1, S, 1))) / s[None, None, :, None]
    return {"hidden_states": bf(hs), "cos": cos, "sin": sin, "Wq": bf(wq), "bq": bf(bq), "grad_out": bf(g)}


def reference(hidden_states, cos, sin, Wq, bq, grad_out):
    g = f64(grad_out)
    c, si = f64(cos)[:, None], f64(sin)[:, None]
    g_nope, g_rope = g[..., :NOPE], g[..., NOPE:]
    d_rope = g_rope * c + rotate_half_t(g_rope * si)
    dq = np.concatenate([g_nope, d_rope], axis=-1).transpose(0, 2, 1, 3).reshape(B * S, NH * QK)
    x = f64(hidden_states).reshape(B * S, HID)
    return mxq(x, 0, "e4m3").T @ mxq(dq, 0, "e5m2")

@@ -1,0 +1,155 @@
+from contextlib import ExitStack
+
+import concourse.mybir as mybir
+
+BF16 = mybir.dt.bfloat16
+F32 = mybir.dt.float32
+U32 = mybir.dt.uint32
+U8 = mybir.dt.uint8
+E4M3_X4 = mybir.dt.float8_e4m3fn_x4
+E5M2_X4 = mybir.dt.float8_e5m2_x4
+ALU = mybir.AluOpType
+
+P = 128
+PACK = 4
+K_PASS = P * PACK
+
+TOKENS = 2048
+HIDDEN = 1024
+HEADS = 8
+NOPE = 64
+ROPE = 128
+HALF = ROPE // 2
+HEAD = NOPE + ROPE
+COLS = HEADS * HEAD
+
+PASSES = TOKENS // K_PASS
+M_TILE = P
+N_TILE = 512
+M_TILES = HIDDEN // M_TILE
+N_TILES = COLS // N_TILE
+MAX_HEADS = -(-N_TILE // HEAD)
+
+FLOPS = 2 * HIDDEN * COLS * TOKENS
+BYTES = 2 * (TOKENS * HIDDEN + TOKENS * COLS + 2 * TOKENS * ROPE) + 4 * HIDDEN * COLS
+
+
+def tile_gptossmlaattention_pb_kernel(tc, hidden_states, cos, sin, Wq, bq, grad_out, out):
+    nc = tc.nc
+    with ExitStack() as ctx:
+        keep = ctx.enter_context(tc.tile_pool(name="keep", bufs=1))
+        x_pool = ctx.enter_context(tc.tile_pool(name="x_pool", bufs=2))
+        g_pool = ctx.enter_context(tc.tile_pool(name="g_pool", bufs=4))
+        prod_pool = ctx.enter_context(tc.tile_pool(name="prod_pool", bufs=2))
+        store_pool = ctx.enter_context(tc.tile_pool(name="store_pool", bufs=4))
+        psum = ctx.enter_context(tc.psum_pool(name="psum", bufs=1))
+
+        x_codes = keep.tile([P, PASSES, HIDDEN], U32, align_bytes=64)
+        x_scales = keep.tile([P, PASSES, HIDDEN], U8, align_bytes=64)
+        dq_codes = keep.tile([P, PASSES, COLS], U32, align_bytes=64)
+        dq_scales = keep.tile([P, PASSES, COLS], U8, align_bytes=64)
+        tables = keep.tile([P, PASSES, 2, PACK, ROPE], BF16)
+        dq_grouped = [
+            keep.tile([P, COLS, PACK], BF16, name="dq_grouped%d" % c, align_bytes=64)
+            for c in range(PASSES)
+        ]
+
+        for n in range(N_TILES):
+            n_cols = slice(n * N_TILE, (n + 1) * N_TILE)
+            first_head = -(-n * N_TILE // HEAD)
+            end_head = -(-(n + 1) * N_TILE // HEAD)
+            heads = end_head - first_head
+
+            acc = [psum.tile([M_TILE, N_TILE], F32, name="acc%d" % m) for m in range(M_TILES)]
+
+            for c in range(PASSES):
+                rows = slice(c * K_PASS, (c + 1) * K_PASS)
+
+                if n == 0:
+                    for q, table in enumerate((cos, sin)):
+                        nc.sync.dma_start(
+                            out=tables[:, c, q].rearrange("p t j -> p (t j)"),
+                            in_=table[0, rows, :].rearrange("(p t) j -> p (t j)", t=PACK),
+                        )
+
+                g = g_pool.tile([P, MAX_HEADS, PACK, HEAD], BF16)
+                nc.sync.dma_start(
+                    out=g[:, 0:heads].rearrange("p h t i -> p h (t i)"),
+                    in_=grad_out[0, first_head:end_head, rows, :].rearrange(
+                        "h (p t) i -> p h (t i)", t=PACK
+                    ),
+                )
+
+                if n == 0:
+                    x_raw = x_pool.tile([P, PACK, HIDDEN], BF16)
+                    nc.sync.dma_start(
+                        out=x_raw[:].rearrange("p t w -> p (t w)"),
+                        in_=hidden_states[0, rows, :].rearrange("(p t) w -> p (t w)", t=PACK),
+                    )
+                    x_grouped = x_pool.tile([P, HIDDEN, PACK], BF16, align_bytes=64)
+                    nc.scalar.copy(
+                        out=x_grouped[:].rearrange("p (w i) t -> p w t i", i=4),
+                        in_=x_raw[:].rearrange("p t (w i) -> p w t i", i=4),
+                    )
+                    nc.vector.quantize_mx(
+                        out=x_codes[:, c, :].bitcast(E4M3_X4),
+                        scales=x_scales[:, c, :],
+                        in_=x_grouped[:].rearrange("p w t -> p (w t)"),
+                    )
+
+                dq_heads = dq_grouped[c][:].rearrange("p (h i) t -> p h i t", i=HEAD)[
+                    :, first_head:end_head
+                ]
+
+                nc.scalar.copy(
+                    out=dq_heads[:, :, 0:NOPE, :],
+                    in_=g[:, 0:heads, :, 0:NOPE].rearrange("p h t i -> p h i t"),
+                )
+
+                prod = prod_pool.tile([P, MAX_HEADS, 2, ROPE, PACK], F32)
+                r = g[:, 0:heads, :, NOPE:HEAD].rearrange("p h t j -> p h j t")
+                for q in range(2):
+                    nc.vector.tensor_tensor(
+                        out=prod[:, 0:heads, q],
+                        in0=r,
+                        in1=tables[:, c, q]
+                        .rearrange("p t j -> p j t")
+                        .unsqueeze(1)
+                        .to_broadcast([P, heads, ROPE, PACK]),
+                        op=ALU.mult,
+                    )
+                nc.vector.tensor_tensor(
+                    out=dq_heads[:, :, NOPE : NOPE + HALF, :],
+                    in0=prod[:, 0:heads, 0, 0:HALF, :],
+                    in1=prod[:, 0:heads, 1, HALF:ROPE, :],
+                    op=ALU.add,
+                )
+                nc.vector.tensor_tensor(
+                    out=dq_heads[:, :, NOPE + HALF : HEAD, :],
+                    in0=prod[:, 0:heads, 0, HALF:ROPE, :],
+                    in1=prod[:, 0:heads, 1, 0:HALF, :],
+                    op=ALU.subtract,
+                )
+
+                nc.vector.quantize_mx(
+                    out=dq_codes[:, c, n_cols].bitcast(E5M2_X4),
+                    scales=dq_scales[:, c, n_cols],
+                    in_=dq_grouped[c][:, n_cols, :].rearrange("p w t -> p (w t)"),
+                )
+
+                for m in range(M_TILES):
+                    m_cols = slice(m * M_TILE, (m + 1) * M_TILE)
+                    nc.tensor.matmul_mx(
+                        out=acc[m][:],
+                        lhsT=x_codes[:, c, m_cols].bitcast(E4M3_X4),
+                        lhsT_scale=x_scales[:, c, m_cols],
+                        rhs=dq_codes[:, c, n_cols].bitcast(E5M2_X4),
+                        rhs_scale=dq_scales[:, c, n_cols],
+                        start=(c == 0),
+                        stop=(c == PASSES - 1),
+                    )
+
+            for m in range(M_TILES):
+                result = store_pool.tile([M_TILE, N_TILE], F32)
+                nc.scalar.copy(out=result[:], in_=acc[m][:])
+                nc.scalar.dma_start(out=out[m * M_TILE : (m + 1) * M_TILE, n_cols], in_=result[:])

@@ -1,6 +1,7 @@
 from contextlib import ExitStack
 
 import concourse.mybir as mybir
+from concourse.masks import make_identity
 
 BF16 = mybir.dt.bfloat16
 F32 = mybir.dt.float32
@@ -30,6 +31,10 @@ M_TILES = HIDDEN // M_TILE
 N_TILES = COLS // N_TILE
 MAX_HEADS = -(-N_TILE // HEAD)
 
+PSUM_BANKS = 8
+COPY_BANKS = 2
+OPEN_GROUPS = PSUM_BANKS - COPY_BANKS
+
 FLOPS = 2 * HIDDEN * COLS * TOKENS
 BYTES = 2 * (TOKENS * HIDDEN + TOKENS * COLS + 2 * TOKENS * ROPE) + 4 * HIDDEN * COLS
 
@@ -40,9 +45,13 @@ def tile_gptossmlaattention_pb_kernel(tc, hidden_states, cos, sin, Wq, bq, grad_
         keep = ctx.enter_context(tc.tile_pool(name="keep", bufs=1))
         x_pool = ctx.enter_context(tc.tile_pool(name="x_pool", bufs=2))
         g_pool = ctx.enter_context(tc.tile_pool(name="g_pool", bufs=4))
-        prod_pool = ctx.enter_context(tc.tile_pool(name="prod_pool", bufs=2))
+        prod_pool = ctx.enter_context(tc.tile_pool(name="prod_pool", bufs=3))
         store_pool = ctx.enter_context(tc.tile_pool(name="store_pool", bufs=4))
-        psum = ctx.enter_context(tc.psum_pool(name="psum", bufs=1))
+        copy_psum = ctx.enter_context(tc.psum_pool(name="copy_psum", bufs=COPY_BANKS))
+        acc_psum = ctx.enter_context(tc.psum_pool(name="acc_psum", bufs=1))
+
+        identity = keep.tile([P, P], BF16)
+        make_identity(nc, identity[:])
 
         x_codes = keep.tile([P, PASSES, HIDDEN], U32, align_bytes=64)
         x_scales = keep.tile([P, PASSES, HIDDEN], U8, align_bytes=64)
@@ -53,103 +62,131 @@ def tile_gptossmlaattention_pb_kernel(tc, hidden_states, cos, sin, Wq, bq, grad_
             keep.tile([P, COLS, PACK], BF16, name="dq_grouped%d" % c, align_bytes=64)
             for c in range(PASSES)
         ]
+        acc = {}
 
-        for n in range(N_TILES):
-            n_cols = slice(n * N_TILE, (n + 1) * N_TILE)
+        def load_tables(c):
+            rows = slice(c * K_PASS, (c + 1) * K_PASS)
+            for q, table in enumerate((cos, sin)):
+                nc.sync.dma_start(
+                    out=tables[:, c, q].rearrange("p t j -> p (t j)"),
+                    in_=table[0, rows, :].rearrange("(p t) j -> p (t j)", t=PACK),
+                )
+
+        def quantise_x(c):
+            rows = slice(c * K_PASS, (c + 1) * K_PASS)
+            x_raw = x_pool.tile([P, PACK, HIDDEN], BF16)
+            nc.sync.dma_start(
+                out=x_raw[:].rearrange("p t w -> p (t w)"),
+                in_=hidden_states[0, rows, :].rearrange("(p t) w -> p (t w)", t=PACK),
+            )
+            x_grouped = x_pool.tile([P, HIDDEN, PACK], BF16, align_bytes=64)
+            nc.scalar.copy(
+                out=x_grouped[:].rearrange("p (w i) t -> p w t i", i=4),
+                in_=x_raw[:].rearrange("p t (w i) -> p w t i", i=4),
+            )
+            nc.vector.quantize_mx(
+                out=x_codes[:, c, :].bitcast(E4M3_X4),
+                scales=x_scales[:, c, :],
+                in_=x_grouped[:].rearrange("p w t -> p (w t)"),
+            )
+
+        def make_dq(n, c):
+            rows = slice(c * K_PASS, (c + 1) * K_PASS)
             first_head = -(-n * N_TILE // HEAD)
             end_head = -(-(n + 1) * N_TILE // HEAD)
             heads = end_head - first_head
 
-            acc = [psum.tile([M_TILE, N_TILE], F32, name="acc%d" % m) for m in range(M_TILES)]
+            g = g_pool.tile([P, MAX_HEADS, PACK, HEAD], BF16)
+            nc.sync.dma_start(
+                out=g[:, 0:heads].rearrange("p h t i -> p h (t i)"),
+                in_=grad_out[0, first_head:end_head, rows, :].rearrange(
+                    "h (p t) i -> p h (t i)", t=PACK
+                ),
+            )
+            dq_heads = dq_grouped[c][:].rearrange("p (h i) t -> p h i t", i=HEAD)[
+                :, first_head:end_head
+            ]
 
-            for c in range(PASSES):
-                rows = slice(c * K_PASS, (c + 1) * K_PASS)
+            nc.scalar.copy(
+                out=dq_heads[:, :, 0:NOPE, :],
+                in_=g[:, 0:heads, :, 0:NOPE].rearrange("p h t i -> p h i t"),
+            )
 
-                if n == 0:
-                    for q, table in enumerate((cos, sin)):
-                        nc.sync.dma_start(
-                            out=tables[:, c, q].rearrange("p t j -> p (t j)"),
-                            in_=table[0, rows, :].rearrange("(p t) j -> p (t j)", t=PACK),
-                        )
-
-                g = g_pool.tile([P, MAX_HEADS, PACK, HEAD], BF16)
-                nc.sync.dma_start(
-                    out=g[:, 0:heads].rearrange("p h t i -> p h (t i)"),
-                    in_=grad_out[0, first_head:end_head, rows, :].rearrange(
-                        "h (p t) i -> p h (t i)", t=PACK
-                    ),
-                )
-
-                if n == 0:
-                    x_raw = x_pool.tile([P, PACK, HIDDEN], BF16)
-                    nc.sync.dma_start(
-                        out=x_raw[:].rearrange("p t w -> p (t w)"),
-                        in_=hidden_states[0, rows, :].rearrange("(p t) w -> p (t w)", t=PACK),
-                    )
-                    x_grouped = x_pool.tile([P, HIDDEN, PACK], BF16, align_bytes=64)
-                    nc.scalar.copy(
-                        out=x_grouped[:].rearrange("p (w i) t -> p w t i", i=4),
-                        in_=x_raw[:].rearrange("p t (w i) -> p w t i", i=4),
-                    )
-                    nc.vector.quantize_mx(
-                        out=x_codes[:, c, :].bitcast(E4M3_X4),
-                        scales=x_scales[:, c, :],
-                        in_=x_grouped[:].rearrange("p w t -> p (w t)"),
-                    )
-
-                dq_heads = dq_grouped[c][:].rearrange("p (h i) t -> p h i t", i=HEAD)[
-                    :, first_head:end_head
-                ]
-
-                nc.scalar.copy(
-                    out=dq_heads[:, :, 0:NOPE, :],
-                    in_=g[:, 0:heads, :, 0:NOPE].rearrange("p h t i -> p h i t"),
-                )
-
-                prod = prod_pool.tile([P, MAX_HEADS, 2, ROPE, PACK], F32)
-                r = g[:, 0:heads, :, NOPE:HEAD].rearrange("p h t j -> p h j t")
-                for q in range(2):
-                    nc.vector.tensor_tensor(
-                        out=prod[:, 0:heads, q],
-                        in0=r,
-                        in1=tables[:, c, q]
-                        .rearrange("p t j -> p j t")
-                        .unsqueeze(1)
-                        .to_broadcast([P, heads, ROPE, PACK]),
-                        op=ALU.mult,
-                    )
-                nc.vector.tensor_tensor(
-                    out=dq_heads[:, :, NOPE : NOPE + HALF, :],
-                    in0=prod[:, 0:heads, 0, 0:HALF, :],
-                    in1=prod[:, 0:heads, 1, HALF:ROPE, :],
-                    op=ALU.add,
+            prod = prod_pool.tile([P, MAX_HEADS, 2, ROPE, PACK], F32)
+            for h in range(heads):
+                r = copy_psum.tile([P, PACK, ROPE], F32)
+                nc.tensor.matmul(
+                    out=r[:], lhsT=identity[:], rhs=g[:, h, :, NOPE:HEAD], start=True, stop=True
                 )
                 nc.vector.tensor_tensor(
-                    out=dq_heads[:, :, NOPE + HALF : HEAD, :],
-                    in0=prod[:, 0:heads, 0, HALF:ROPE, :],
-                    in1=prod[:, 0:heads, 1, 0:HALF, :],
-                    op=ALU.subtract,
+                    out=prod[:, h],
+                    in0=r[:].rearrange("p t j -> p j t").unsqueeze(1).to_broadcast([P, 2, ROPE, PACK]),
+                    in1=tables[:, c].rearrange("p q t j -> p q j t"),
+                    op=ALU.mult,
                 )
+            nc.gpsimd.tensor_tensor(
+                out=dq_heads[:, :, NOPE : NOPE + HALF, :],
+                in0=prod[:, 0:heads, 0, 0:HALF, :],
+                in1=prod[:, 0:heads, 1, HALF:ROPE, :],
+                op=ALU.add,
+            )
+            nc.gpsimd.tensor_tensor(
+                out=dq_heads[:, :, NOPE + HALF : HEAD, :],
+                in0=prod[:, 0:heads, 0, HALF:ROPE, :],
+                in1=prod[:, 0:heads, 1, 0:HALF, :],
+                op=ALU.subtract,
+            )
 
-                nc.vector.quantize_mx(
-                    out=dq_codes[:, c, n_cols].bitcast(E5M2_X4),
-                    scales=dq_scales[:, c, n_cols],
-                    in_=dq_grouped[c][:, n_cols, :].rearrange("p w t -> p (w t)"),
-                )
+        def mx_pass(n, c, m):
+            n_cols = slice(n * N_TILE, (n + 1) * N_TILE)
+            m_cols = slice(m * M_TILE, (m + 1) * M_TILE)
+            nc.tensor.matmul_mx(
+                out=acc[m][:],
+                lhsT=x_codes[:, c, m_cols].bitcast(E4M3_X4),
+                lhsT_scale=x_scales[:, c, m_cols],
+                rhs=dq_codes[:, c, n_cols].bitcast(E5M2_X4),
+                rhs_scale=dq_scales[:, c, n_cols],
+                start=(c == 0),
+                stop=(c == PASSES - 1),
+            )
 
-                for m in range(M_TILES):
-                    m_cols = slice(m * M_TILE, (m + 1) * M_TILE)
-                    nc.tensor.matmul_mx(
-                        out=acc[m][:],
-                        lhsT=x_codes[:, c, m_cols].bitcast(E4M3_X4),
-                        lhsT_scale=x_scales[:, c, m_cols],
-                        rhs=dq_codes[:, c, n_cols].bitcast(E5M2_X4),
-                        rhs_scale=dq_scales[:, c, n_cols],
-                        start=(c == 0),
-                        stop=(c == PASSES - 1),
-                    )
+        def open_bank(m):
+            acc[m] = acc_psum.tile([M_TILE, N_TILE], F32, name="acc%d" % (m % OPEN_GROUPS))
 
-            for m in range(M_TILES):
-                result = store_pool.tile([M_TILE, N_TILE], F32)
-                nc.scalar.copy(out=result[:], in_=acc[m][:])
-                nc.scalar.dma_start(out=out[m * M_TILE : (m + 1) * M_TILE, n_cols], in_=result[:])
+        def store(n, m):
+            result = store_pool.tile([M_TILE, N_TILE], F32)
+            nc.scalar.copy(out=result[:], in_=acc[m][:])
+            nc.scalar.dma_start(
+                out=out[m * M_TILE : (m + 1) * M_TILE, n * N_TILE : (n + 1) * N_TILE], in_=result[:]
+            )
+
+        def multiply(n, c):
+            n_cols = slice(n * N_TILE, (n + 1) * N_TILE)
+            nc.vector.quantize_mx(
+                out=dq_codes[:, c, n_cols].bitcast(E5M2_X4),
+                scales=dq_scales[:, c, n_cols],
+                in_=dq_grouped[c][:, n_cols, :].rearrange("p w t -> p (w t)"),
+            )
+            for m in range(OPEN_GROUPS):
+                if c == 0:
+                    open_bank(m)
+                mx_pass(n, c, m)
+            if c == PASSES - 1:
+                for m in range(OPEN_GROUPS):
+                    store(n, m)
+                for m in range(OPEN_GROUPS, M_TILES):
+                    open_bank(m)
+                    for every_c in range(PASSES):
+                        mx_pass(n, every_c, m)
+                    store(n, m)
+
+        steps = [(n, c) for n in range(N_TILES) for c in range(PASSES)]
+        for i, (n, c) in enumerate(steps):
+            if n == 0:
+                load_tables(c)
+            make_dq(n, c)
+            if n == 0:
+                quantise_x(c)
+            if i > 0:
+                multiply(*steps[i - 1])
+        multiply(*steps[-1])

@@ -32,8 +32,8 @@ N_TILES = COLS // N_TILE
 MAX_HEADS = -(-N_TILE // HEAD)
 
 PSUM_BANKS = 8
-COPY_BANKS = 2
-OPEN_GROUPS = PSUM_BANKS - COPY_BANKS
+TABLE_BANKS = 2
+OPEN_GROUPS = PSUM_BANKS - TABLE_BANKS
 
 FLOPS = 2 * HIDDEN * COLS * TOKENS
 BYTES = 2 * (TOKENS * HIDDEN + TOKENS * COLS + 2 * TOKENS * ROPE) + 4 * HIDDEN * COLS
@@ -47,7 +47,7 @@ def tile_gptossmlaattention_pb_kernel(tc, hidden_states, cos, sin, Wq, bq, grad_
         g_pool = ctx.enter_context(tc.tile_pool(name="g_pool", bufs=4))
         prod_pool = ctx.enter_context(tc.tile_pool(name="prod_pool", bufs=3))
         store_pool = ctx.enter_context(tc.tile_pool(name="store_pool", bufs=4))
-        copy_psum = ctx.enter_context(tc.psum_pool(name="copy_psum", bufs=COPY_BANKS))
+        table_psum = ctx.enter_context(tc.psum_pool(name="table_psum", bufs=TABLE_BANKS))
         acc_psum = ctx.enter_context(tc.psum_pool(name="acc_psum", bufs=1))
 
         identity = keep.tile([P, P], BF16)
@@ -63,6 +63,8 @@ def tile_gptossmlaattention_pb_kernel(tc, hidden_states, cos, sin, Wq, bq, grad_
             for c in range(PASSES)
         ]
         acc = {}
+        x_grouped = {}
+        table_bank = {}
 
         def load_tables(c):
             rows = slice(c * K_PASS, (c + 1) * K_PASS)
@@ -72,22 +74,28 @@ def tile_gptossmlaattention_pb_kernel(tc, hidden_states, cos, sin, Wq, bq, grad_
                     in_=table[0, rows, :].rearrange("(p t) j -> p (t j)", t=PACK),
                 )
 
-        def quantise_x(c):
+        def copy_tables(n, c):
+            table_bank[(n, c)] = table_psum.tile([P, 2, PACK, ROPE], BF16, name="table_bank")
+            for q in range(2):
+                nc.tensor.matmul(
+                    out=table_bank[(n, c)][:, q],
+                    lhsT=identity[:],
+                    rhs=tables[:, c, q],
+                    start=True,
+                    stop=True,
+                )
+
+        def regroup_x(c):
             rows = slice(c * K_PASS, (c + 1) * K_PASS)
             x_raw = x_pool.tile([P, PACK, HIDDEN], BF16)
             nc.sync.dma_start(
                 out=x_raw[:].rearrange("p t w -> p (t w)"),
                 in_=hidden_states[0, rows, :].rearrange("(p t) w -> p (t w)", t=PACK),
             )
-            x_grouped = x_pool.tile([P, HIDDEN, PACK], BF16, align_bytes=64)
+            x_grouped[c] = x_pool.tile([P, HIDDEN, PACK], BF16, name="x_grouped", align_bytes=64)
             nc.scalar.copy(
-                out=x_grouped[:].rearrange("p (w i) t -> p w t i", i=4),
+                out=x_grouped[c][:].rearrange("p (w i) t -> p w t i", i=4),
                 in_=x_raw[:].rearrange("p t (w i) -> p w t i", i=4),
-            )
-            nc.vector.quantize_mx(
-                out=x_codes[:, c, :].bitcast(E4M3_X4),
-                scales=x_scales[:, c, :],
-                in_=x_grouped[:].rearrange("p w t -> p (w t)"),
             )
 
         def make_dq(n, c):
@@ -113,24 +121,24 @@ def tile_gptossmlaattention_pb_kernel(tc, hidden_states, cos, sin, Wq, bq, grad_
             )
 
             prod = prod_pool.tile([P, MAX_HEADS, 2, ROPE, PACK], F32)
-            for h in range(heads):
-                r = copy_psum.tile([P, PACK, ROPE], F32)
-                nc.tensor.matmul(
-                    out=r[:], lhsT=identity[:], rhs=g[:, h, :, NOPE:HEAD], start=True, stop=True
-                )
+            for q in range(2):
                 nc.vector.tensor_tensor(
-                    out=prod[:, h],
-                    in0=r[:].rearrange("p t j -> p j t").unsqueeze(1).to_broadcast([P, 2, ROPE, PACK]),
-                    in1=tables[:, c].rearrange("p q t j -> p q j t"),
+                    out=prod[:, 0:heads, q],
+                    in0=g[:, 0:heads, :, NOPE:HEAD].rearrange("p h t j -> p h j t"),
+                    in1=table_bank[(n, c)][:, q]
+                    .rearrange("p t j -> p j t")
+                    .unsqueeze(1)
+                    .to_broadcast([P, heads, ROPE, PACK]),
                     op=ALU.mult,
                 )
-            nc.gpsimd.tensor_tensor(
+            adder = nc.vector if (n, c) == steps[-1] else nc.gpsimd
+            adder.tensor_tensor(
                 out=dq_heads[:, :, NOPE : NOPE + HALF, :],
                 in0=prod[:, 0:heads, 0, 0:HALF, :],
                 in1=prod[:, 0:heads, 1, HALF:ROPE, :],
                 op=ALU.add,
             )
-            nc.gpsimd.tensor_tensor(
+            adder.tensor_tensor(
                 out=dq_heads[:, :, NOPE + HALF : HEAD, :],
                 in0=prod[:, 0:heads, 0, HALF:ROPE, :],
                 in1=prod[:, 0:heads, 1, 0:HALF, :],
@@ -150,18 +158,36 @@ def tile_gptossmlaattention_pb_kernel(tc, hidden_states, cos, sin, Wq, bq, grad_
                 stop=(c == PASSES - 1),
             )
 
-        def open_bank(m):
-            acc[m] = acc_psum.tile([M_TILE, N_TILE], F32, name="acc%d" % (m % OPEN_GROUPS))
+        def open_bank(n, m):
+            if m >= OPEN_GROUPS and n == N_TILES - 1:
+                acc[m] = table_psum.tile([M_TILE, N_TILE], F32, name="table_bank")
+            else:
+                acc[m] = acc_psum.tile([M_TILE, N_TILE], F32, name="acc%d" % (m % OPEN_GROUPS))
 
         def store(n, m):
             result = store_pool.tile([M_TILE, N_TILE], F32)
-            nc.scalar.copy(out=result[:], in_=acc[m][:])
-            nc.scalar.dma_start(
-                out=out[m * M_TILE : (m + 1) * M_TILE, n * N_TILE : (n + 1) * N_TILE], in_=result[:]
-            )
+            out_tile = out[m * M_TILE : (m + 1) * M_TILE, n * N_TILE : (n + 1) * N_TILE]
+            if n == N_TILES - 1 and m % 2 == 1:
+                nc.vector.tensor_copy(out=result[:], in_=acc[m][:])
+                nc.sync.dma_start(out=out_tile, in_=result[:])
+            else:
+                nc.scalar.copy(out=result[:], in_=acc[m][:])
+                nc.scalar.dma_start(out=out_tile, in_=result[:])
+
+        def begin_late_rows(n):
+            for m in range(OPEN_GROUPS, M_TILES):
+                open_bank(n, m)
+                for c in range(PASSES - 1):
+                    mx_pass(n, c, m)
 
         def multiply(n, c):
             n_cols = slice(n * N_TILE, (n + 1) * N_TILE)
+            if n == 0:
+                nc.vector.quantize_mx(
+                    out=x_codes[:, c, :].bitcast(E4M3_X4),
+                    scales=x_scales[:, c, :],
+                    in_=x_grouped[c][:].rearrange("p w t -> p (w t)"),
+                )
             nc.vector.quantize_mx(
                 out=dq_codes[:, c, n_cols].bitcast(E5M2_X4),
                 scales=dq_scales[:, c, n_cols],
@@ -169,24 +195,29 @@ def tile_gptossmlaattention_pb_kernel(tc, hidden_states, cos, sin, Wq, bq, grad_
             )
             for m in range(OPEN_GROUPS):
                 if c == 0:
-                    open_bank(m)
+                    open_bank(n, m)
                 mx_pass(n, c, m)
             if c == PASSES - 1:
                 for m in range(OPEN_GROUPS):
                     store(n, m)
+                if n < N_TILES - 1:
+                    begin_late_rows(n)
                 for m in range(OPEN_GROUPS, M_TILES):
-                    open_bank(m)
-                    for every_c in range(PASSES):
-                        mx_pass(n, every_c, m)
+                    mx_pass(n, c, m)
                     store(n, m)
 
         steps = [(n, c) for n in range(N_TILES) for c in range(PASSES)]
+        load_tables(0)
+        copy_tables(*steps[0])
         for i, (n, c) in enumerate(steps):
-            if n == 0:
-                load_tables(c)
             make_dq(n, c)
+            if n == 0 and c + 1 < PASSES:
+                load_tables(c + 1)
+            if i + 1 < len(steps):
+                copy_tables(*steps[i + 1])
             if n == 0:
-                quantise_x(c)
+                regroup_x(c)
             if i > 0:
                 multiply(*steps[i - 1])
+        begin_late_rows(N_TILES - 1)
         multiply(*steps[-1])

@@ -46,7 +46,7 @@ def tile_gptossmlaattention_pb_kernel(tc, hidden_states, cos, sin, Wq, bq, grad_
         x_pool = ctx.enter_context(tc.tile_pool(name="x_pool", bufs=2))
         g_pool = ctx.enter_context(tc.tile_pool(name="g_pool", bufs=4))
         prod_pool = ctx.enter_context(tc.tile_pool(name="prod_pool", bufs=3))
-        store_pool = ctx.enter_context(tc.tile_pool(name="store_pool", bufs=4))
+        store_pool = ctx.enter_context(tc.tile_pool(name="store_pool", bufs=M_TILES))
         table_psum = ctx.enter_context(tc.psum_pool(name="table_psum", bufs=TABLE_BANKS))
         acc_psum = ctx.enter_context(tc.psum_pool(name="acc_psum", bufs=1))
 
@@ -92,7 +92,7 @@ def tile_gptossmlaattention_pb_kernel(tc, hidden_states, cos, sin, Wq, bq, grad_
                 out=x_raw[:].rearrange("p t w -> p (t w)"),
                 in_=hidden_states[0, rows, :].rearrange("(p t) w -> p (t w)", t=PACK),
             )
-            x_grouped[c] = x_pool.tile([P, HIDDEN, PACK], BF16, name="x_grouped", align_bytes=64)
+            x_grouped[c] = x_pool.tile([P, HIDDEN, PACK], BF16, name="x_grouped", bufs=3, align_bytes=64)
             nc.scalar.copy(
                 out=x_grouped[c][:].rearrange("p (w i) t -> p w t i", i=4),
                 in_=x_raw[:].rearrange("p t (w i) -> p w t i", i=4),
@@ -180,19 +180,23 @@ def tile_gptossmlaattention_pb_kernel(tc, hidden_states, cos, sin, Wq, bq, grad_
                 for c in range(PASSES - 1):
                     mx_pass(n, c, m)
 
-        def multiply(n, c):
+        def quantise_dq(n, c):
             n_cols = slice(n * N_TILE, (n + 1) * N_TILE)
+            nc.vector.quantize_mx(
+                out=dq_codes[:, c, n_cols].bitcast(E5M2_X4),
+                scales=dq_scales[:, c, n_cols],
+                in_=dq_grouped[c][:, n_cols, :].rearrange("p w t -> p (w t)"),
+            )
+
+        def multiply(n, c):
             if n == 0:
                 nc.vector.quantize_mx(
                     out=x_codes[:, c, :].bitcast(E4M3_X4),
                     scales=x_scales[:, c, :],
                     in_=x_grouped[c][:].rearrange("p w t -> p (w t)"),
                 )
-            nc.vector.quantize_mx(
-                out=dq_codes[:, c, n_cols].bitcast(E5M2_X4),
-                scales=dq_scales[:, c, n_cols],
-                in_=dq_grouped[c][:, n_cols, :].rearrange("p w t -> p (w t)"),
-            )
+            if (n, c) == steps[-1]:
+                begin_late_rows(n)
             for m in range(OPEN_GROUPS):
                 if c == 0:
                     open_bank(n, m)
@@ -209,15 +213,17 @@ def tile_gptossmlaattention_pb_kernel(tc, hidden_states, cos, sin, Wq, bq, grad_
         steps = [(n, c) for n in range(N_TILES) for c in range(PASSES)]
         load_tables(0)
         copy_tables(*steps[0])
-        for i, (n, c) in enumerate(steps):
-            make_dq(n, c)
-            if n == 0 and c + 1 < PASSES:
-                load_tables(c + 1)
-            if i + 1 < len(steps):
-                copy_tables(*steps[i + 1])
-            if n == 0:
-                regroup_x(c)
-            if i > 0:
-                multiply(*steps[i - 1])
-        begin_late_rows(N_TILES - 1)
-        multiply(*steps[-1])
+        for i in range(len(steps) + 2):
+            if i < len(steps):
+                n, c = steps[i]
+                make_dq(n, c)
+                if n == 0 and c + 1 < PASSES:
+                    load_tables(c + 1)
+                if i + 1 < len(steps):
+                    copy_tables(*steps[i + 1])
+                if n == 0:
+                    regroup_x(c)
+            if 1 <= i <= len(steps):
+                quantise_dq(*steps[i - 1])
+            if i >= 2:
+                multiply(*steps[i - 2])

@@ -65,6 +65,7 @@ def tile_gptossmlaattention_pb_kernel(tc, hidden_states, cos, sin, Wq, bq, grad_
         acc = {}
         x_grouped = {}
         table_bank = {}
+        grad = {}
 
         def load_tables(c):
             rows = slice(c * K_PASS, (c + 1) * K_PASS)
@@ -98,27 +99,34 @@ def tile_gptossmlaattention_pb_kernel(tc, hidden_states, cos, sin, Wq, bq, grad_
                 in_=x_raw[:].rearrange("p t (w i) -> p w t i", i=4),
             )
 
-        def make_dq(n, c):
+        def load_grad(n, c):
             rows = slice(c * K_PASS, (c + 1) * K_PASS)
             first_head = -(-n * N_TILE // HEAD)
             end_head = -(-(n + 1) * N_TILE // HEAD)
-            heads = end_head - first_head
-
-            g = g_pool.tile([P, MAX_HEADS, PACK, HEAD], BF16)
+            grad[(n, c)] = g_pool.tile([P, MAX_HEADS, PACK, HEAD], BF16, name="grad")
             nc.sync.dma_start(
-                out=g[:, 0:heads].rearrange("p h t i -> p h (t i)"),
+                out=grad[(n, c)][:, 0 : end_head - first_head].rearrange("p h t i -> p h (t i)"),
                 in_=grad_out[0, first_head:end_head, rows, :].rearrange(
                     "h (p t) i -> p h (t i)", t=PACK
                 ),
             )
+
+            dq_heads = dq_grouped[c][:].rearrange("p (h i) t -> p h i t", i=HEAD)
+            nc.scalar.copy(
+                out=dq_heads[:, first_head:end_head, 0:NOPE, :],
+                in_=grad[(n, c)][:, 0 : end_head - first_head, :, 0:NOPE].rearrange(
+                    "p h t i -> p h i t"
+                ),
+            )
+
+        def rotate(n, c):
+            first_head = -(-n * N_TILE // HEAD)
+            end_head = -(-(n + 1) * N_TILE // HEAD)
+            heads = end_head - first_head
+            g = grad[(n, c)]
             dq_heads = dq_grouped[c][:].rearrange("p (h i) t -> p h i t", i=HEAD)[
                 :, first_head:end_head
             ]
-
-            nc.scalar.copy(
-                out=dq_heads[:, :, 0:NOPE, :],
-                in_=g[:, 0:heads, :, 0:NOPE].rearrange("p h t i -> p h i t"),
-            )
 
             prod = prod_pool.tile([P, MAX_HEADS, 2, ROPE, PACK], F32)
             for q in range(2):
@@ -210,19 +218,21 @@ def tile_gptossmlaattention_pb_kernel(tc, hidden_states, cos, sin, Wq, bq, grad_
                     mx_pass(n, c, m)
                     store(n, m)
 
+        def prepare(n, c):
+            if n == 0:
+                load_tables(c)
+            load_grad(n, c)
+            copy_tables(n, c)
+
         steps = [(n, c) for n in range(N_TILES) for c in range(PASSES)]
-        load_tables(0)
-        copy_tables(*steps[0])
+        prepare(*steps[0])
         for i in range(len(steps) + 2):
+            if i + 1 < len(steps):
+                prepare(*steps[i + 1])
             if i < len(steps):
-                n, c = steps[i]
-                make_dq(n, c)
-                if n == 0 and c + 1 < PASSES:
-                    load_tables(c + 1)
-                if i + 1 < len(steps):
-                    copy_tables(*steps[i + 1])
-                if n == 0:
-                    regroup_x(c)
+                rotate(*steps[i])
+            if i < PASSES:
+                regroup_x(i)
             if 1 <= i <= len(steps):
                 quantise_dq(*steps[i - 1])
             if i >= 2:

@@ -66,6 +66,7 @@ def tile_gptossmlaattention_pb_kernel(tc, hidden_states, cos, sin, Wq, bq, grad_
         x_grouped = {}
         table_bank = {}
         grad = {}
+        prods = {}
 
         def load_tables(c):
             rows = slice(c * K_PASS, (c + 1) * K_PASS)
@@ -99,10 +100,18 @@ def tile_gptossmlaattention_pb_kernel(tc, hidden_states, cos, sin, Wq, bq, grad_
                 in_=x_raw[:].rearrange("p t (w i) -> p w t i", i=4),
             )
 
+        def nope_heads(n):
+            return -(-n * N_TILE // HEAD), -(-(n + 1) * N_TILE // HEAD)
+
+        def rope_heads(n):
+            return -(-(n * N_TILE - NOPE) // HEAD), -(-((n + 1) * N_TILE - NOPE) // HEAD)
+
+        def loaded_heads(n):
+            return min(nope_heads(n)[0], rope_heads(n)[0]), max(nope_heads(n)[1], rope_heads(n)[1])
+
         def load_grad(n, c):
             rows = slice(c * K_PASS, (c + 1) * K_PASS)
-            first_head = -(-n * N_TILE // HEAD)
-            end_head = -(-(n + 1) * N_TILE // HEAD)
+            first_head, end_head = loaded_heads(n)
             grad[(n, c)] = g_pool.tile([P, MAX_HEADS, PACK, HEAD], BF16, name="grad")
             nc.sync.dma_start(
                 out=grad[(n, c)][:, 0 : end_head - first_head].rearrange("p h t i -> p h (t i)"),
@@ -111,34 +120,41 @@ def tile_gptossmlaattention_pb_kernel(tc, hidden_states, cos, sin, Wq, bq, grad_
                 ),
             )
 
+            first_nope, end_nope = nope_heads(n)
             dq_heads = dq_grouped[c][:].rearrange("p (h i) t -> p h i t", i=HEAD)
             nc.scalar.copy(
-                out=dq_heads[:, first_head:end_head, 0:NOPE, :],
-                in_=grad[(n, c)][:, 0 : end_head - first_head, :, 0:NOPE].rearrange(
-                    "p h t i -> p h i t"
-                ),
+                out=dq_heads[:, first_nope:end_nope, 0:NOPE, :],
+                in_=grad[(n, c)][
+                    :, first_nope - first_head : end_nope - first_head, :, 0:NOPE
+                ].rearrange("p h t i -> p h i t"),
             )
 
-        def rotate(n, c):
-            first_head = -(-n * N_TILE // HEAD)
-            end_head = -(-(n + 1) * N_TILE // HEAD)
+        def products(n, c):
+            first_head, end_head = rope_heads(n)
             heads = end_head - first_head
+            skip = first_head - loaded_heads(n)[0]
             g = grad[(n, c)]
-            dq_heads = dq_grouped[c][:].rearrange("p (h i) t -> p h i t", i=HEAD)[
-                :, first_head:end_head
-            ]
 
             prod = prod_pool.tile([P, MAX_HEADS, 2, ROPE, PACK], F32)
+            prods[(n, c)] = prod
             for q in range(2):
                 nc.vector.tensor_tensor(
                     out=prod[:, 0:heads, q],
-                    in0=g[:, 0:heads, :, NOPE:HEAD].rearrange("p h t j -> p h j t"),
+                    in0=g[:, skip : skip + heads, :, NOPE:HEAD].rearrange("p h t j -> p h j t"),
                     in1=table_bank[(n, c)][:, q]
                     .rearrange("p t j -> p j t")
                     .unsqueeze(1)
                     .to_broadcast([P, heads, ROPE, PACK]),
                     op=ALU.mult,
                 )
+
+        def sums(n, c):
+            first_head, end_head = rope_heads(n)
+            heads = end_head - first_head
+            prod = prods[(n, c)]
+            dq_heads = dq_grouped[c][:].rearrange("p (h i) t -> p h i t", i=HEAD)[
+                :, first_head:end_head
+            ]
             adder = nc.vector if (n, c) == steps[-1] else nc.gpsimd
             adder.tensor_tensor(
                 out=dq_heads[:, :, NOPE : NOPE + HALF, :],
@@ -230,10 +246,14 @@ def tile_gptossmlaattention_pb_kernel(tc, hidden_states, cos, sin, Wq, bq, grad_
             if i + 1 < len(steps):
                 prepare(*steps[i + 1])
             if i < len(steps):
-                rotate(*steps[i])
+                products(*steps[i])
+            if i < len(steps) - 1:
+                sums(*steps[i])
             if i < PASSES:
                 regroup_x(i)
             if 1 <= i <= len(steps):
                 quantise_dq(*steps[i - 1])
+            if i == len(steps) - 1:
+                sums(*steps[i])
             if i >= 2:
                 multiply(*steps[i - 2])

@@ -77,10 +77,10 @@ def tile_gptossmlaattention_pb_kernel(tc, hidden_states, cos, sin, Wq, bq, grad_
                 )
 
         def copy_tables(n, c):
-            table_bank[(n, c)] = table_psum.tile([P, 2, PACK, ROPE], BF16, name="table_bank")
+            table_bank[(n, c)] = table_psum.tile([P, 2, ROPE, PACK], BF16, name="table_bank")
             for q in range(2):
                 nc.tensor.matmul(
-                    out=table_bank[(n, c)][:, q],
+                    out=table_bank[(n, c)][:, q].rearrange("p j t -> p t j"),
                     lhsT=identity[:],
                     rhs=tables[:, c, q],
                     start=True,
@@ -142,7 +142,6 @@ def tile_gptossmlaattention_pb_kernel(tc, hidden_states, cos, sin, Wq, bq, grad_
                     out=prod[:, 0:heads, q],
                     in0=g[:, skip : skip + heads, :, NOPE:HEAD].rearrange("p h t j -> p h j t"),
                     in1=table_bank[(n, c)][:, q]
-                    .rearrange("p t j -> p j t")
                     .unsqueeze(1)
                     .to_broadcast([P, heads, ROPE, PACK]),
                     op=ALU.mult,

@@ -240,6 +240,10 @@ def tile_gptossmlaattention_pb_kernel(tc, hidden_states, cos, sin, Wq, bq, grad_
             copy_tables(n, c)
 
         steps = [(n, c) for n in range(N_TILES) for c in range(PASSES)]
+        quantise_turn = [
+            j + (2 if steps[j][1] == 0 and steps[j][0] != 1 or steps[j] == (1, 1) else 1)
+            for j in range(len(steps))
+        ]
         prepare(*steps[0])
         for i in range(len(steps) + 2):
             if i + 1 < len(steps):
@@ -250,8 +254,9 @@ def tile_gptossmlaattention_pb_kernel(tc, hidden_states, cos, sin, Wq, bq, grad_
                 sums(*steps[i])
             if i < PASSES:
                 regroup_x(i)
-            if 1 <= i <= len(steps):
-                quantise_dq(*steps[i - 1])
+            for j in range(len(steps)):
+                if quantise_turn[j] == i:
+                    quantise_dq(*steps[j])
             if i == len(steps) - 1:
                 sums(*steps[i])
             if i >= 2:

@@ -42,11 +42,11 @@ BYTES = 2 * (TOKENS * HIDDEN + TOKENS * COLS + 2 * TOKENS * ROPE) + 4 * HIDDEN *
 def tile_gptossmlaattention_pb_kernel(tc, hidden_states, cos, sin, Wq, bq, grad_out, out):
     nc = tc.nc
     with ExitStack() as ctx:
-        keep = ctx.enter_context(tc.tile_pool(name="keep", bufs=1))
-        x_pool = ctx.enter_context(tc.tile_pool(name="x_pool", bufs=2))
-        g_pool = ctx.enter_context(tc.tile_pool(name="g_pool", bufs=4))
-        prod_pool = ctx.enter_context(tc.tile_pool(name="prod_pool", bufs=3))
         store_pool = ctx.enter_context(tc.tile_pool(name="store_pool", bufs=M_TILES))
+        prod_pool = ctx.enter_context(tc.tile_pool(name="prod_pool", bufs=3))
+        g_pool = ctx.enter_context(tc.tile_pool(name="g_pool", bufs=4))
+        x_pool = ctx.enter_context(tc.tile_pool(name="x_pool", bufs=2))
+        keep = ctx.enter_context(tc.tile_pool(name="keep", bufs=1))
         table_psum = ctx.enter_context(tc.psum_pool(name="table_psum", bufs=TABLE_BANKS))
         acc_psum = ctx.enter_context(tc.psum_pool(name="acc_psum", bufs=1))
 

from contextlib import ExitStack

import concourse.mybir as mybir
from concourse.masks import make_identity

BF16 = mybir.dt.bfloat16
F32 = mybir.dt.float32
U32 = mybir.dt.uint32
U8 = mybir.dt.uint8
E4M3_X4 = mybir.dt.float8_e4m3fn_x4
E5M2_X4 = mybir.dt.float8_e5m2_x4
ALU = mybir.AluOpType

P = 128
PACK = 4
K_PASS = P * PACK

TOKENS = 2048
HIDDEN = 1024
HEADS = 8
NOPE = 64
ROPE = 128
HALF = ROPE // 2
HEAD = NOPE + ROPE
COLS = HEADS * HEAD

PASSES = TOKENS // K_PASS
M_TILE = P
N_TILE = 512
M_TILES = HIDDEN // M_TILE
N_TILES = COLS // N_TILE
MAX_HEADS = -(-N_TILE // HEAD)

PSUM_BANKS = 8
TABLE_BANKS = 2
OPEN_GROUPS = PSUM_BANKS - TABLE_BANKS

FLOPS = 2 * HIDDEN * COLS * TOKENS
BYTES = 2 * (TOKENS * HIDDEN + TOKENS * COLS + 2 * TOKENS * ROPE) + 4 * HIDDEN * COLS


def tile_gptossmlaattention_pb_kernel(tc, hidden_states, cos, sin, Wq, bq, grad_out, out):
    nc = tc.nc
    with ExitStack() as ctx:
        store_pool = ctx.enter_context(tc.tile_pool(name="store_pool", bufs=M_TILES))
        prod_pool = ctx.enter_context(tc.tile_pool(name="prod_pool", bufs=3))
        g_pool = ctx.enter_context(tc.tile_pool(name="g_pool", bufs=4))
        x_pool = ctx.enter_context(tc.tile_pool(name="x_pool", bufs=2))
        keep = ctx.enter_context(tc.tile_pool(name="keep", bufs=1))
        table_psum = ctx.enter_context(tc.psum_pool(name="table_psum", bufs=TABLE_BANKS))
        acc_psum = ctx.enter_context(tc.psum_pool(name="acc_psum", bufs=1))

        identity = keep.tile([P, P], BF16)
        make_identity(nc, identity[:])

        x_codes = keep.tile([P, PASSES, HIDDEN], U32, align_bytes=64)
        x_scales = keep.tile([P, PASSES, HIDDEN], U8, align_bytes=64)
        dq_codes = keep.tile([P, PASSES, COLS], U32, align_bytes=64)
        dq_scales = keep.tile([P, PASSES, COLS], U8, align_bytes=64)
        tables = keep.tile([P, PASSES, 2, PACK, ROPE], BF16)
        dq_grouped = [
            keep.tile([P, COLS, PACK], BF16, name="dq_grouped%d" % c, align_bytes=64)
            for c in range(PASSES)
        ]
        acc = {}
        x_grouped = {}
        table_bank = {}
        grad = {}
        prods = {}

        def load_tables(c):
            rows = slice(c * K_PASS, (c + 1) * K_PASS)
            for q, table in enumerate((cos, sin)):
                nc.sync.dma_start(
                    out=tables[:, c, q].rearrange("p t j -> p (t j)"),
                    in_=table[0, rows, :].rearrange("(p t) j -> p (t j)", t=PACK),
                )

        def copy_tables(n, c):
            table_bank[(n, c)] = table_psum.tile([P, 2, ROPE, PACK], BF16, name="table_bank")
            for q in range(2):
                nc.tensor.matmul(
                    out=table_bank[(n, c)][:, q].rearrange("p j t -> p t j"),
                    lhsT=identity[:],
                    rhs=tables[:, c, q],
                    start=True,
                    stop=True,
                )

        def regroup_x(c):
            rows = slice(c * K_PASS, (c + 1) * K_PASS)
            x_raw = x_pool.tile([P, PACK, HIDDEN], BF16)
            nc.sync.dma_start(
                out=x_raw[:].rearrange("p t w -> p (t w)"),
                in_=hidden_states[0, rows, :].rearrange("(p t) w -> p (t w)", t=PACK),
            )
            x_grouped[c] = x_pool.tile([P, HIDDEN, PACK], BF16, name="x_grouped", bufs=3, align_bytes=64)
            nc.scalar.copy(
                out=x_grouped[c][:].rearrange("p (w i) t -> p w t i", i=4),
                in_=x_raw[:].rearrange("p t (w i) -> p w t i", i=4),
            )

        def nope_heads(n):
            return -(-n * N_TILE // HEAD), -(-(n + 1) * N_TILE // HEAD)

        def rope_heads(n):
            return -(-(n * N_TILE - NOPE) // HEAD), -(-((n + 1) * N_TILE - NOPE) // HEAD)

        def loaded_heads(n):
            return min(nope_heads(n)[0], rope_heads(n)[0]), max(nope_heads(n)[1], rope_heads(n)[1])

        def load_grad(n, c):
            rows = slice(c * K_PASS, (c + 1) * K_PASS)
            first_head, end_head = loaded_heads(n)
            grad[(n, c)] = g_pool.tile([P, MAX_HEADS, PACK, HEAD], BF16, name="grad")
            nc.sync.dma_start(
                out=grad[(n, c)][:, 0 : end_head - first_head].rearrange("p h t i -> p h (t i)"),
                in_=grad_out[0, first_head:end_head, rows, :].rearrange(
                    "h (p t) i -> p h (t i)", t=PACK
                ),
            )

            first_nope, end_nope = nope_heads(n)
            dq_heads = dq_grouped[c][:].rearrange("p (h i) t -> p h i t", i=HEAD)
            nc.scalar.copy(
                out=dq_heads[:, first_nope:end_nope, 0:NOPE, :],
                in_=grad[(n, c)][
                    :, first_nope - first_head : end_nope - first_head, :, 0:NOPE
                ].rearrange("p h t i -> p h i t"),
            )

        def products(n, c):
            first_head, end_head = rope_heads(n)
            heads = end_head - first_head
            skip = first_head - loaded_heads(n)[0]
            g = grad[(n, c)]

            prod = prod_pool.tile([P, MAX_HEADS, 2, ROPE, PACK], F32)
            prods[(n, c)] = prod
            for q in range(2):
                nc.vector.tensor_tensor(
                    out=prod[:, 0:heads, q],
                    in0=g[:, skip : skip + heads, :, NOPE:HEAD].rearrange("p h t j -> p h j t"),
                    in1=table_bank[(n, c)][:, q]
                    .unsqueeze(1)
                    .to_broadcast([P, heads, ROPE, PACK]),
                    op=ALU.mult,
                )

        def sums(n, c):
            first_head, end_head = rope_heads(n)
            heads = end_head - first_head
            prod = prods[(n, c)]
            dq_heads = dq_grouped[c][:].rearrange("p (h i) t -> p h i t", i=HEAD)[
                :, first_head:end_head
            ]
            adder = nc.vector if (n, c) == steps[-1] else nc.gpsimd
            adder.tensor_tensor(
                out=dq_heads[:, :, NOPE : NOPE + HALF, :],
                in0=prod[:, 0:heads, 0, 0:HALF, :],
                in1=prod[:, 0:heads, 1, HALF:ROPE, :],
                op=ALU.add,
            )
            adder.tensor_tensor(
                out=dq_heads[:, :, NOPE + HALF : HEAD, :],
                in0=prod[:, 0:heads, 0, HALF:ROPE, :],
                in1=prod[:, 0:heads, 1, 0:HALF, :],
                op=ALU.subtract,
            )

        def mx_pass(n, c, m):
            n_cols = slice(n * N_TILE, (n + 1) * N_TILE)
            m_cols = slice(m * M_TILE, (m + 1) * M_TILE)
            nc.tensor.matmul_mx(
                out=acc[m][:],
                lhsT=x_codes[:, c, m_cols].bitcast(E4M3_X4),
                lhsT_scale=x_scales[:, c, m_cols],
                rhs=dq_codes[:, c, n_cols].bitcast(E5M2_X4),
                rhs_scale=dq_scales[:, c, n_cols],
                start=(c == 0),
                stop=(c == PASSES - 1),
            )

        def open_bank(n, m):
            if m >= OPEN_GROUPS and n == N_TILES - 1:
                acc[m] = table_psum.tile([M_TILE, N_TILE], F32, name="table_bank")
            else:
                acc[m] = acc_psum.tile([M_TILE, N_TILE], F32, name="acc%d" % (m % OPEN_GROUPS))

        def store(n, m):
            result = store_pool.tile([M_TILE, N_TILE], F32)
            out_tile = out[m * M_TILE : (m + 1) * M_TILE, n * N_TILE : (n + 1) * N_TILE]
            if n == N_TILES - 1 and m % 2 == 1:
                nc.vector.tensor_copy(out=result[:], in_=acc[m][:])
                nc.sync.dma_start(out=out_tile, in_=result[:])
            else:
                nc.scalar.copy(out=result[:], in_=acc[m][:])
                nc.scalar.dma_start(out=out_tile, in_=result[:])

        def begin_late_rows(n):
            for m in range(OPEN_GROUPS, M_TILES):
                open_bank(n, m)
                for c in range(PASSES - 1):
                    mx_pass(n, c, m)

        def quantise_dq(n, c):
            n_cols = slice(n * N_TILE, (n + 1) * N_TILE)
            nc.vector.quantize_mx(
                out=dq_codes[:, c, n_cols].bitcast(E5M2_X4),
                scales=dq_scales[:, c, n_cols],
                in_=dq_grouped[c][:, n_cols, :].rearrange("p w t -> p (w t)"),
            )

        def multiply(n, c):
            if n == 0:
                nc.vector.quantize_mx(
                    out=x_codes[:, c, :].bitcast(E4M3_X4),
                    scales=x_scales[:, c, :],
                    in_=x_grouped[c][:].rearrange("p w t -> p (w t)"),
                )
            if (n, c) == steps[-1]:
                begin_late_rows(n)
            for m in range(OPEN_GROUPS):
                if c == 0:
                    open_bank(n, m)
                mx_pass(n, c, m)
            if c == PASSES - 1:
                for m in range(OPEN_GROUPS):
                    store(n, m)
                if n < N_TILES - 1:
                    begin_late_rows(n)
                for m in range(OPEN_GROUPS, M_TILES):
                    mx_pass(n, c, m)
                    store(n, m)

        def prepare(n, c):
            if n == 0:
                load_tables(c)
            load_grad(n, c)
            copy_tables(n, c)

        steps = [(n, c) for n in range(N_TILES) for c in range(PASSES)]
        quantise_turn = [
            j + (2 if steps[j][1] == 0 and steps[j][0] != 1 or steps[j] == (1, 1) else 1)
            for j in range(len(steps))
        ]
        prepare(*steps[0])
        for i in range(len(steps) + 2):
            if i + 1 < len(steps):
                prepare(*steps[i + 1])
            if i < len(steps):
                products(*steps[i])
            if i < len(steps) - 1:
                sums(*steps[i])
            if i < PASSES:
                regroup_x(i)
            for j in range(len(steps)):
                if quantise_turn[j] == i:
                    quantise_dq(*steps[j])
            if i == len(steps) - 1:
                sums(*steps[i])
            if i >= 2:
                multiply(*steps[i - 2])
